import numpy as np
import ml_dtypes


def mxq(x, axis, fmt="e4m3"):
    dtype, down = {"e4m3": (ml_dtypes.float8_e4m3fn, 7), "e5m2": (ml_dtypes.float8_e5m2, 14)}[fmt]
    v = np.moveaxis(np.asarray(x, np.float32).astype(ml_dtypes.bfloat16).astype(np.float64), axis, -1)
    blocks = v.reshape(v.shape[:-1] + (-1, 32))
    amax = np.abs(blocks).max(-1, keepdims=True)
    byte = np.maximum(np.where(amax > 0, np.frexp(amax)[1] - 1 + 127, 0) - down, 1)
    scale = np.exp2(byte - 127.0)
    codes = (blocks / scale).astype(np.float32).astype(dtype).astype(np.float64)
    return np.moveaxis((codes * scale).reshape(v.shape), -1, axis)


WIDE = False


def mx_kscale(k):
    if not WIDE:
        return np.ones(k)
    levels = np.array([10, -10, 5, -5, 0])
    a = np.random.permutation(np.resize(levels, k // 512 * 4)).reshape(k // 512, 4)
    idx = np.arange(k)
    return np.exp2(a[idx // 512, idx % 128 // 32])


BF16 = ml_dtypes.bfloat16


def bf(x):
    return np.asarray(x, np.float32).astype(BF16)


def f64(x):
    return np.asarray(x).astype(np.float64)


B, S, D, F, P, NQ = 2, 128, 1024, 1024, 1024, 3
LN_EPS = 1e-5


def layernorm(v, g, b):
    m = v.mean(-1, keepdims=True)
    var = v.var(-1, keepdims=True)
    return (v - m) / np.sqrt(var + LN_EPS) * g + b


def setup_inputs():
    s = mx_kscale(P)
    return {"in_proto": bf(np.random.standard_normal((NQ, F, P)) * s),
            "pt_w": bf(np.random.standard_normal((NQ, D, P)) / np.sqrt(P) / s),
            "pln_g": bf(1.0 + 0.1 * np.random.standard_normal((NQ, D))),
            "pln_b": bf(0.1 * np.random.standard_normal((NQ, D))),
            "proto_w": bf(np.random.standard_normal((NQ, F, D)) * 0.5)}


def reference(in_proto, pt_w, pln_g, pln_b, proto_w):
    prc = mxq(f64(in_proto), 2, "e4m3") @ mxq(f64(pt_w), 2, "e4m3").transpose(0, 2, 1)
    return f64(proto_w) + layernorm(prc, f64(pln_g)[:, None, :], f64(pln_b)[:, None, :])

@@ -1,0 +1,242 @@
+from contextlib import ExitStack
+
+import concourse.mybir as mybir
+from concourse.masks import make_identity
+
+F32 = mybir.dt.float32
+BF16 = mybir.dt.bfloat16
+U32 = mybir.dt.uint32
+U8 = mybir.dt.uint8
+I32 = mybir.dt.int32
+FP8X4 = mybir.dt.float8_e4m3fn_x4
+ACT = mybir.ActivationFunctionType
+ALU = mybir.AluOpType
+
+NB = 3
+D = 1024
+P = 128
+LN_EPS = 1e-5
+FLOPS = 2 * NB * D * D * D
+
+RAW_BUFS = 4
+LEAD = 6
+C_AHEAD = 2
+COPY_V_HEAD = True
+N_PE_C = 13
+
+
+def tile_moietransformerblock_pb_kernel(tc, in_proto, pt_w, pln_g, pln_b, proto_w, out):
+    nc = tc.nc
+    a_view = in_proto.rearrange("n (p t) k -> n p t k", t=8)
+    w_view = pt_w.rearrange("n (t p) k -> n p t k", p=P)
+    pw_view = proto_w.rearrange("n (p t) d -> n p t d", t=8)
+    out_view = out.rearrange("n (p t) d -> n p t d", t=8)
+
+    with ExitStack() as ctx:
+        const = ctx.enter_context(tc.tile_pool(name="const", bufs=1))
+        rawp = ctx.enter_context(tc.tile_pool(name="rawp", bufs=RAW_BUFS))
+        pwp = ctx.enter_context(tc.tile_pool(name="pwp", bufs=3))
+        grpp = ctx.enter_context(tc.tile_pool(name="grpp", bufs=4))
+        codep = ctx.enter_context(tc.tile_pool(name="codep", bufs=2))
+        xsp = ctx.enter_context(tc.tile_pool(name="xsp", bufs=3))
+        tp = ctx.enter_context(tc.tile_pool(name="tp", bufs=4))
+        cp = ctx.enter_context(tc.tile_pool(name="cp", bufs=4))
+        smallp = ctx.enter_context(tc.tile_pool(name="smallp", bufs=4))
+        psum_t = ctx.enter_context(tc.psum_pool(name="psum_t", bufs=2))
+        psum_c = ctx.enter_context(tc.psum_pool(name="psum_c", bufs=2))
+        psum_x = ctx.enter_context(tc.psum_pool(name="psum_x", bufs=4))
+
+        stage = const.tile([1, 2 * NB * D], BF16, name="stage")
+        nc.scalar.dma_start(out=stage[0:1, 0 : NB * D], in_=pln_g.rearrange("(o n) d -> o (n d)", o=1))
+        nc.scalar.dma_start(out=stage[0:1, NB * D : 2 * NB * D], in_=pln_b.rearrange("(o n) d -> o (n d)", o=1))
+        ident = const.tile([P, P], F32, name="ident")
+        make_identity(nc, ident[:])
+        identb = const.tile([P, P], BF16, name="identb")
+        make_identity(nc, identb[:])
+        ones = const.tile([P, P], BF16, name="ones")
+        nc.vector.memset(ones[:], 1.0)
+        mhalf = const.tile([P, 1], F32, name="mhalf")
+        nc.vector.memset(mhalf[:], -0.5)
+        gpad = const.tile([P, NB * D], BF16, name="gpad")
+        bpad = const.tile([P, NB * D], BF16, name="bpad")
+        nc.vector.memset(gpad[:].bitcast(I32), 0)
+        nc.vector.memset(bpad[:].bitcast(I32), 0)
+        nc.vector.tensor_copy(out=gpad[0:1, :], in_=stage[0:1, 0 : NB * D])
+        nc.vector.tensor_copy(out=bpad[0:1, :], in_=stage[0:1, NB * D : 2 * NB * D])
+        g_all = const.tile([P, NB * D], BF16, name="g_all")
+        b_all = const.tile([P, NB * D], BF16, name="b_all")
+        junk = const.tile([P, D], BF16, name="junk")
+
+        raw = {}
+        pw_raw = {}
+
+        def load_chunk(c):
+            n, r = divmod(c, 4)
+            view = w_view if r < 2 else a_view
+            j = r % 2
+            t_raw = rawp.tile([P, 4 * D], BF16, name="raw%d" % c, tag="raw")
+            nc.sync.dma_start(
+                out=t_raw[:].rearrange("p (t k) -> p t k", t=4),
+                in_=view[n][:, 4 * j : 4 * j + 4, :],
+            )
+            raw[c] = t_raw
+
+        def load_pw(k):
+            n, j = divmod(k, 2)
+            t_pw = pwp.tile([P, 4 * D], BF16, name="pw%d" % k, tag="pw")
+            nc.sync.dma_start(
+                out=t_pw[:].rearrange("p (t k) -> p t k", t=4),
+                in_=pw_view[n][:, 4 * j : 4 * j + 4, :],
+            )
+            pw_raw[k] = t_pw
+
+        def broadcast(n):
+            for src, dst, eng in ((gpad, g_all, 0), (bpad, b_all, 1)):
+                for h in range(2):
+                    cols = slice(n * D + 512 * h, n * D + 512 * h + 512)
+                    ps = psum_t.tile([P, 512], F32, name="bc", tag="tr")
+                    nc.tensor.matmul(ps[:], lhsT=ones[:], rhs=src[:, cols], start=True, stop=True)
+                    if eng == 0 and n == 0:
+                        nc.vector.tensor_copy(out=dst[:, cols], in_=ps[:])
+                    else:
+                        nc.scalar.copy(out=dst[:, cols], in_=ps[:])
+
+        codes = {}
+
+        def unit_front(u):
+            c, g = divmod(u, 2)
+            n, r = divmod(c, 4)
+            op = 0 if r < 2 else 1
+            j = r % 2
+            if (n, op) not in codes:
+                cd = codep.tile([P, 2, D], U32, name="cd%d_%d" % (n, op), tag="cd%d" % op, align_bytes=64)
+                sc = codep.tile([P, 2, D], U8, name="sc%d_%d" % (n, op), tag="sc%d" % op, align_bytes=64)
+                codes[(n, op)] = (cd, sc)
+            words = raw[c][:].bitcast(F32)
+            grp = grpp.tile([P, 2048], BF16, name="grp%d" % u, tag="grp", align_bytes=64)
+            grp_w = grp[:].bitcast(F32).rearrange("p (a r w) -> p a r w", a=4, w=2)
+            for h in range(2):
+                ps = psum_t.tile([P, 2, 2, P], F32, name="tr", tag="tr")
+                for tl in range(2):
+                    for w in range(2):
+                        col = 512 * (2 * h + tl) + 256 * g + 128 * w
+                        nc.tensor.transpose(ps[:, tl, w, :], words[:, col : col + 128], ident[:])
+                src = ps[:].rearrange("p a w r -> p a r w")
+                dst = grp_w[:, 2 * h : 2 * h + 2]
+                if COPY_V_HEAD and u < LEAD and h == 1:
+                    nc.vector.tensor_copy(out=dst, in_=src)
+                else:
+                    nc.scalar.copy(out=dst, in_=src)
+            return (n, op, g, j, grp)
+
+        def unit_back(info):
+            n, op, g, j, grp = info
+            cd, sc = codes[(n, op)]
+            cols = slice(512 * j, 512 * j + 512)
+            nc.vector.quantize_mx(out=cd[:, g, cols].bitcast(FP8X4), scales=sc[:, g, cols], in_=grp[:])
+
+        c_tiles = {}
+
+        def make_c(s):
+            n, i = divmod(s, 8)
+            k, tl = divmod(s, 4)
+            c_t = cp.tile([P, D], F32, name="c%d" % s, tag="c")
+            lo = 512 if s < N_PE_C else 0
+            nc.vector.tensor_tensor(
+                out=c_t[:, lo:D], in0=pw_raw[k][:, tl * D + lo : (tl + 1) * D], in1=b_all[:, n * D + lo : (n + 1) * D], op=ALU.add
+            )
+            c_tiles[s] = c_t
+
+        def make_c_pe(s):
+            n, i = divmod(s, 8)
+            k, tl = divmod(s, 4)
+            c_ps = psum_c.tile([P, 512], F32, name="cps", tag="cps")
+            nc.tensor.matmul(c_ps[:], lhsT=identb[:], rhs=pw_raw[k][:, tl * D : tl * D + 512], start=True, stop=False)
+            nc.tensor.matmul(c_ps[:], lhsT=ones[:], rhs=bpad[:, n * D : n * D + 512], start=False, stop=True)
+            return c_ps
+
+        load_chunk(0)
+        load_chunk(1)
+        load_chunk(2)
+        load_pw(0)
+        load_chunk(3)
+        next_chunk = 4
+        pending = None
+        for u in range(LEAD):
+            info = unit_front(u)
+            if pending is not None:
+                unit_back(pending)
+            pending = info
+            if u % 2 == 1:
+                load_chunk(next_chunk)
+                next_chunk += 1
+            if u == 1:
+                broadcast(0)
+        unit_back(pending)
+        pending = None
+        load_pw(1)
+        for s in range(C_AHEAD):
+            make_c(s)
+
+        for s in range(8 * NB):
+            n, i = divmod(s, 8)
+            cd_w, sc_w = codes[(n, 0)]
+            cd_a, sc_a = codes[(n, 1)]
+            rows = slice(P * i, P * i + P)
+            xs = xsp.tile([P, D], F32, name="xs%d" % s, tag="xs")
+            sums = smallp.tile([P, 2], F32, name="sums%d" % s, tag="sums")
+            for h in range(2):
+                cols = slice(512 * h, 512 * h + 512)
+                x_ps = psum_x.tile([P, 512], F32, name="x", tag="x")
+                for g in range(2):
+                    nc.tensor.matmul_mx(
+                        out=x_ps[:],
+                        lhsT=cd_a[:, g, rows].bitcast(FP8X4),
+                        lhsT_scale=sc_a[:, g, rows],
+                        rhs=cd_w[:, g, cols].bitcast(FP8X4),
+                        rhs_scale=sc_w[:, g, cols],
+                        start=(g == 0),
+                        stop=(g == 1),
+                    )
+                nc.scalar.activation(out=xs[:, cols], in_=x_ps[:], func=ACT.Copy, accum_out=sums[:, h : h + 1])
+            c_ps = make_c_pe(s) if s < N_PE_C else None
+            u = s + LEAD
+            info = unit_front(u) if u < 8 * NB else None
+            negmean = smallp.tile([P, 1], F32, name="nm%d" % s, tag="nm")
+            nc.gpsimd.tensor_scalar(
+                out=negmean[:], in0=sums[:, 0:1], scalar1=sums[:, 1:2], scalar2=-1.0 / D, op0=ALU.add, op1=ALU.mult
+            )
+            ssq = smallp.tile([P, 1], F32, name="ssq%d" % s, tag="ssq")
+            nc.scalar.activation(out=junk[:], in_=xs[:], func=ACT.Square, bias=negmean[:], scale=1.0, accum_out=ssq[:])
+            t_t = tp.tile([P, D], F32, name="t%d" % s, tag="t")
+            nc.vector.scalar_tensor_tensor(
+                out=t_t[:], in0=xs[:], scalar=negmean[:], in1=g_all[:, n * D : (n + 1) * D], op0=ALU.add, op1=ALU.mult
+            )
+            if info is not None:
+                unit_back(info)
+                if u % 2 == 1 and next_chunk < 4 * NB:
+                    load_chunk(next_chunk)
+                    next_chunk += 1
+            var = smallp.tile([P, 1], F32, name="var%d" % s, tag="var")
+            nc.gpsimd.tensor_scalar(out=var[:], in0=ssq[:], scalar1=1.0 / D, scalar2=LN_EPS, op0=ALU.mult, op1=ALU.add)
+            rstd = smallp.tile([P, 1], F32, name="rstd%d" % s, tag="rstd")
+            nc.gpsimd.tensor_tensor(out=rstd[:], in0=var[:], in1=mhalf[:], op=ALU.pow)
+            if c_ps is not None:
+                nc.vector.scalar_tensor_tensor(
+                    out=t_t[:, 0:512], in0=t_t[:, 0:512], scalar=rstd[:], in1=c_ps[:], op0=ALU.mult, op1=ALU.add
+                )
+                nc.vector.scalar_tensor_tensor(
+                    out=t_t[:, 512:D], in0=t_t[:, 512:D], scalar=rstd[:], in1=c_tiles[s][:, 512:D], op0=ALU.mult, op1=ALU.add
+                )
+            else:
+                nc.vector.scalar_tensor_tensor(
+                    out=t_t[:], in0=t_t[:], scalar=rstd[:], in1=c_tiles[s][:], op0=ALU.mult, op1=ALU.add
+                )
+            nc.sync.dma_start(out=out_view[n][:, i, :], in_=t_t[:])
+            if s in (1, 9):
+                broadcast(s // 8 + 1)
+            s2 = s + C_AHEAD
+            if s2 < 8 * NB:
+                if s2 % 4 == 0 and s2 // 4 + 1 < 2 * NB:
+                    load_pw(s2 // 4 + 1)
+                make_c(s2)

@@ -15,14 +15,25 @@ ALU = mybir.AluOpType
 NB = 3
 D = 1024
 P = 128
+H = 512
 LN_EPS = 1e-5
 FLOPS = 2 * NB * D * D * D
 
-RAW_BUFS = 4
-LEAD = 6
+N_SLOTS = 8 * NB
+N_UNITS = 8 * NB
+HEAD_UNITS = 6
 C_AHEAD = 2
-COPY_V_HEAD = True
-N_PE_C = 13
+PE_C_SLOTS = tuple(range(11, 24))
+V_COPY_UNITS = (19, 21, 23)
+PINNED = True
+
+
+def units_of_slot(s):
+    if s == 0:
+        return [6]
+    if s == 1:
+        return [7, 8]
+    return [s + 7] if s + 7 < N_UNITS else []
 
 
 def tile_moietransformerblock_pb_kernel(tc, in_proto, pt_w, pln_g, pln_b, proto_w, out):
@@ -33,14 +44,16 @@ def tile_moietransformerblock_pb_kernel(tc, in_proto, pt_w, pln_g, pln_b, proto_
     out_view = out.rearrange("n (p t) d -> n p t d", t=8)
 
     with ExitStack() as ctx:
+        if PINNED:
+            ctx.enter_context(tc.manual_schedule())
         const = ctx.enter_context(tc.tile_pool(name="const", bufs=1))
-        rawp = ctx.enter_context(tc.tile_pool(name="rawp", bufs=RAW_BUFS))
+        rawp = ctx.enter_context(tc.tile_pool(name="rawp", bufs=4))
         pwp = ctx.enter_context(tc.tile_pool(name="pwp", bufs=3))
         grpp = ctx.enter_context(tc.tile_pool(name="grpp", bufs=4))
         codep = ctx.enter_context(tc.tile_pool(name="codep", bufs=2))
         xsp = ctx.enter_context(tc.tile_pool(name="xsp", bufs=3))
-        tp = ctx.enter_context(tc.tile_pool(name="tp", bufs=4))
-        cp = ctx.enter_context(tc.tile_pool(name="cp", bufs=4))
+        tpool = ctx.enter_context(tc.tile_pool(name="tpool", bufs=4))
+        cpool = ctx.enter_context(tc.tile_pool(name="cpool", bufs=4))
         smallp = ctx.enter_context(tc.tile_pool(name="smallp", bufs=4))
         psum_t = ctx.enter_context(tc.psum_pool(name="psum_t", bufs=2))
         psum_c = ctx.enter_context(tc.psum_pool(name="psum_c", bufs=2))
@@ -53,22 +66,26 @@ def tile_moietransformerblock_pb_kernel(tc, in_proto, pt_w, pln_g, pln_b, proto_
         make_identity(nc, ident[:])
         identb = const.tile([P, P], BF16, name="identb")
         make_identity(nc, identb[:])
+        eps = const.tile([P, 1], F32, name="eps")
+        nc.vector.memset(eps[:], LN_EPS)
+        warm = const.tile([P, 1], F32, name="warm")
+        nc.scalar.activation(out=warm[:], in_=eps[:], func=ACT.Abs_reciprocal_sqrt, bias=eps[:], scale=1.0)
         ones = const.tile([P, P], BF16, name="ones")
         nc.vector.memset(ones[:], 1.0)
-        mhalf = const.tile([P, 1], F32, name="mhalf")
-        nc.vector.memset(mhalf[:], -0.5)
         gpad = const.tile([P, NB * D], BF16, name="gpad")
         bpad = const.tile([P, NB * D], BF16, name="bpad")
         nc.vector.memset(gpad[:].bitcast(I32), 0)
         nc.vector.memset(bpad[:].bitcast(I32), 0)
-        nc.vector.tensor_copy(out=gpad[0:1, :], in_=stage[0:1, 0 : NB * D])
-        nc.vector.tensor_copy(out=bpad[0:1, :], in_=stage[0:1, NB * D : 2 * NB * D])
         g_all = const.tile([P, NB * D], BF16, name="g_all")
         b_all = const.tile([P, NB * D], BF16, name="b_all")
         junk = const.tile([P, D], BF16, name="junk")
+        junk2 = const.tile([P, 2], F32, name="junk2")
 
         raw = {}
         pw_raw = {}
+        codes = {}
+        c_tiles = {}
+        state = {}
 
         def load_chunk(c):
             n, r = divmod(c, 4)
@@ -90,18 +107,16 @@ def tile_moietransformerblock_pb_kernel(tc, in_proto, pt_w, pln_g, pln_b, proto_
             )
             pw_raw[k] = t_pw
 
-        def broadcast(n):
-            for src, dst, eng in ((gpad, g_all, 0), (bpad, b_all, 1)):
-                for h in range(2):
-                    cols = slice(n * D + 512 * h, n * D + 512 * h + 512)
-                    ps = psum_t.tile([P, 512], F32, name="bc", tag="tr")
-                    nc.tensor.matmul(ps[:], lhsT=ones[:], rhs=src[:, cols], start=True, stop=True)
-                    if eng == 0 and n == 0:
-                        nc.vector.tensor_copy(out=dst[:, cols], in_=ps[:])
-                    else:
-                        nc.scalar.copy(out=dst[:, cols], in_=ps[:])
-
-        codes = {}
+        def broadcast(n, which):
+            src, dst = ((gpad, g_all), (bpad, b_all))[which]
+            for h in range(2):
+                cols = slice(n * D + H * h, n * D + H * h + H)
+                ps = psum_t.tile([P, H], F32, name="bc", tag="tr")
+                nc.tensor.matmul(ps[:], lhsT=ones[:], rhs=src[:, cols], start=True, stop=True)
+                if h == 0:
+                    nc.scalar.copy(out=dst[:, cols], in_=ps[:])
+                else:
+                    nc.vector.tensor_copy(out=dst[:, cols], in_=ps[:])
 
         def unit_front(u):
             c, g = divmod(u, 2)
@@ -119,78 +134,103 @@ def tile_moietransformerblock_pb_kernel(tc, in_proto, pt_w, pln_g, pln_b, proto_
                 ps = psum_t.tile([P, 2, 2, P], F32, name="tr", tag="tr")
                 for tl in range(2):
                     for w in range(2):
-                        col = 512 * (2 * h + tl) + 256 * g + 128 * w
-                        nc.tensor.transpose(ps[:, tl, w, :], words[:, col : col + 128], ident[:])
+                        col = H * (2 * h + tl) + 256 * g + P * w
+                        nc.tensor.transpose(ps[:, tl, w, :], words[:, col : col + P], ident[:])
                 src = ps[:].rearrange("p a w r -> p a r w")
                 dst = grp_w[:, 2 * h : 2 * h + 2]
-                if COPY_V_HEAD and u < LEAD and h == 1:
+                if h == 1 and (u < HEAD_UNITS or u in V_COPY_UNITS):
                     nc.vector.tensor_copy(out=dst, in_=src)
                 else:
                     nc.scalar.copy(out=dst, in_=src)
+            if g == 1 and c + 4 < 4 * NB:
+                load_chunk(c + 4)
             return (n, op, g, j, grp)
 
         def unit_back(info):
             n, op, g, j, grp = info
             cd, sc = codes[(n, op)]
-            cols = slice(512 * j, 512 * j + 512)
+            cols = slice(H * j, H * j + H)
             nc.vector.quantize_mx(out=cd[:, g, cols].bitcast(FP8X4), scales=sc[:, g, cols], in_=grp[:])
 
-        c_tiles = {}
-
         def make_c(s):
-            n, i = divmod(s, 8)
+            n = s // 8
             k, tl = divmod(s, 4)
-            c_t = cp.tile([P, D], F32, name="c%d" % s, tag="c")
-            lo = 512 if s < N_PE_C else 0
+            c_t = cpool.tile([P, D], F32, name="c%d" % s, tag="c")
+            lo = H if s in PE_C_SLOTS else 0
             nc.vector.tensor_tensor(
-                out=c_t[:, lo:D], in0=pw_raw[k][:, tl * D + lo : (tl + 1) * D], in1=b_all[:, n * D + lo : (n + 1) * D], op=ALU.add
+                out=c_t[:, lo:D],
+                in0=pw_raw[k][:, tl * D + lo : (tl + 1) * D],
+                in1=b_all[:, n * D + lo : (n + 1) * D],
+                op=ALU.add,
             )
             c_tiles[s] = c_t
 
         def make_c_pe(s):
-            n, i = divmod(s, 8)
+            n = s // 8
             k, tl = divmod(s, 4)
-            c_ps = psum_c.tile([P, 512], F32, name="cps", tag="cps")
-            nc.tensor.matmul(c_ps[:], lhsT=identb[:], rhs=pw_raw[k][:, tl * D : tl * D + 512], start=True, stop=False)
-            nc.tensor.matmul(c_ps[:], lhsT=ones[:], rhs=bpad[:, n * D : n * D + 512], start=False, stop=True)
+            c_ps = psum_c.tile([P, H], F32, name="cps", tag="cps")
+            nc.tensor.matmul(c_ps[:], lhsT=identb[:], rhs=pw_raw[k][:, tl * D : tl * D + H], start=True, stop=False)
+            nc.tensor.matmul(c_ps[:], lhsT=ones[:], rhs=bpad[:, n * D : n * D + H], start=False, stop=True)
             return c_ps
+
+        def finish(s):
+            n, i = divmod(s, 8)
+            t_t, rstd, c_ps = state[s]
+            if c_ps is not None:
+                nc.vector.scalar_tensor_tensor(
+                    out=t_t[:, 0:H], in0=t_t[:, 0:H], scalar=rstd[:], in1=c_ps[:], op0=ALU.mult, op1=ALU.add
+                )
+                nc.vector.scalar_tensor_tensor(
+                    out=t_t[:, H:D], in0=t_t[:, H:D], scalar=rstd[:], in1=c_tiles[s][:, H:D], op0=ALU.mult, op1=ALU.add
+                )
+            else:
+                nc.vector.scalar_tensor_tensor(
+                    out=t_t[:], in0=t_t[:], scalar=rstd[:], in1=c_tiles[s][:], op0=ALU.mult, op1=ALU.add
+                )
+            nc.sync.dma_start(out=out_view[n][:, i, :], in_=t_t[:])
+
+        def make_rstd(s):
+            t_t, ssq, c_ps = state[s]
+            rstd = smallp.tile([P, 1], F32, name="rstd%d" % s, tag="rstd")
+            nc.scalar.activation(out=rstd[:], in_=ssq[:], func=ACT.Abs_reciprocal_sqrt, bias=eps[:], scale=1.0 / D)
+            state[s] = (t_t, rstd, c_ps)
 
         load_chunk(0)
         load_chunk(1)
         load_chunk(2)
         load_pw(0)
         load_chunk(3)
-        next_chunk = 4
         pending = None
-        for u in range(LEAD):
+        for u in range(HEAD_UNITS):
             info = unit_front(u)
             if pending is not None:
                 unit_back(pending)
             pending = info
-            if u % 2 == 1:
-                load_chunk(next_chunk)
-                next_chunk += 1
             if u == 1:
-                broadcast(0)
+                nc.vector.tensor_copy(out=gpad[0:1, :], in_=stage[0:1, 0 : NB * D])
+                nc.vector.tensor_copy(out=bpad[0:1, :], in_=stage[0:1, NB * D : 2 * NB * D])
+            if u == 3:
+                broadcast(0, 0)
+                broadcast(0, 1)
+                load_pw(1)
         unit_back(pending)
-        pending = None
-        load_pw(1)
         for s in range(C_AHEAD):
             make_c(s)
 
-        for s in range(8 * NB):
+        for s in range(N_SLOTS):
             n, i = divmod(s, 8)
             cd_w, sc_w = codes[(n, 0)]
             cd_a, sc_a = codes[(n, 1)]
             rows = slice(P * i, P * i + P)
             xs = xsp.tile([P, D], F32, name="xs%d" % s, tag="xs")
             sums = smallp.tile([P, 2], F32, name="sums%d" % s, tag="sums")
+            x_ps = []
             for h in range(2):
-                cols = slice(512 * h, 512 * h + 512)
-                x_ps = psum_x.tile([P, 512], F32, name="x", tag="x")
+                cols = slice(H * h, H * h + H)
+                x_h = psum_x.tile([P, H], F32, name="x", tag="x")
                 for g in range(2):
                     nc.tensor.matmul_mx(
-                        out=x_ps[:],
+                        out=x_h[:],
                         lhsT=cd_a[:, g, rows].bitcast(FP8X4),
                         lhsT_scale=sc_a[:, g, rows],
                         rhs=cd_w[:, g, cols].bitcast(FP8X4),
@@ -198,45 +238,35 @@ def tile_moietransformerblock_pb_kernel(tc, in_proto, pt_w, pln_g, pln_b, proto_
                         start=(g == 0),
                         stop=(g == 1),
                     )
-                nc.scalar.activation(out=xs[:, cols], in_=x_ps[:], func=ACT.Copy, accum_out=sums[:, h : h + 1])
-            c_ps = make_c_pe(s) if s < N_PE_C else None
-            u = s + LEAD
-            info = unit_front(u) if u < 8 * NB else None
+                x_ps.append(x_h)
+            nc.scalar.activation(out=xs[:, 0:H], in_=x_ps[0][:], func=ACT.Copy, accum_out=sums[:, 0:1])
+            if s > 0:
+                make_rstd(s - 1)
+            nc.scalar.activation(out=xs[:, H:D], in_=x_ps[1][:], func=ACT.Copy, accum_out=sums[:, 1:2])
+            if s > 0:
+                finish(s - 1)
+            if s + C_AHEAD < N_SLOTS:
+                make_c(s + C_AHEAD)
+            c_ps = make_c_pe(s) if s in PE_C_SLOTS else None
+            infos = [unit_front(u) for u in units_of_slot(s)]
             negmean = smallp.tile([P, 1], F32, name="nm%d" % s, tag="nm")
-            nc.gpsimd.tensor_scalar(
-                out=negmean[:], in0=sums[:, 0:1], scalar1=sums[:, 1:2], scalar2=-1.0 / D, op0=ALU.add, op1=ALU.mult
-            )
-            ssq = smallp.tile([P, 1], F32, name="ssq%d" % s, tag="ssq")
-            nc.scalar.activation(out=junk[:], in_=xs[:], func=ACT.Square, bias=negmean[:], scale=1.0, accum_out=ssq[:])
-            t_t = tp.tile([P, D], F32, name="t%d" % s, tag="t")
+            nc.scalar.activation(out=junk2[:], in_=sums[:], func=ACT.Copy, scale=-1.0 / D, accum_out=negmean[:])
+            t_t = tpool.tile([P, D], F32, name="t%d" % s, tag="t")
             nc.vector.scalar_tensor_tensor(
                 out=t_t[:], in0=xs[:], scalar=negmean[:], in1=g_all[:, n * D : (n + 1) * D], op0=ALU.add, op1=ALU.mult
             )
-            if info is not None:
+            ssq = smallp.tile([P, 1], F32, name="ssq%d" % s, tag="ssq")
+            nc.scalar.activation(out=junk[:], in_=xs[:], func=ACT.Square, bias=negmean[:], scale=1.0, accum_out=ssq[:])
+            state[s] = (t_t, ssq, c_ps)
+            for info in infos:
                 unit_back(info)
-                if u % 2 == 1 and next_chunk < 4 * NB:
-                    load_chunk(next_chunk)
-                    next_chunk += 1
-            var = smallp.tile([P, 1], F32, name="var%d" % s, tag="var")
-            nc.gpsimd.tensor_scalar(out=var[:], in0=ssq[:], scalar1=1.0 / D, scalar2=LN_EPS, op0=ALU.mult, op1=ALU.add)
-            rstd = smallp.tile([P, 1], F32, name="rstd%d" % s, tag="rstd")
-            nc.gpsimd.tensor_tensor(out=rstd[:], in0=var[:], in1=mhalf[:], op=ALU.pow)
-            if c_ps is not None:
-                nc.vector.scalar_tensor_tensor(
-                    out=t_t[:, 0:512], in0=t_t[:, 0:512], scalar=rstd[:], in1=c_ps[:], op0=ALU.mult, op1=ALU.add
-                )
-                nc.vector.scalar_tensor_tensor(
-                    out=t_t[:, 512:D], in0=t_t[:, 512:D], scalar=rstd[:], in1=c_tiles[s][:, 512:D], op0=ALU.mult, op1=ALU.add
-                )
-            else:
-                nc.vector.scalar_tensor_tensor(
-                    out=t_t[:], in0=t_t[:], scalar=rstd[:], in1=c_tiles[s][:], op0=ALU.mult, op1=ALU.add
-                )
-            nc.sync.dma_start(out=out_view[n][:, i, :], in_=t_t[:])
-            if s in (1, 9):
-                broadcast(s // 8 + 1)
-            s2 = s + C_AHEAD
-            if s2 < 8 * NB:
-                if s2 % 4 == 0 and s2 // 4 + 1 < 2 * NB:
-                    load_pw(s2 // 4 + 1)
-                make_c(s2)
+            if s in (2, 10):
+                broadcast(s // 8 + 1, 0)
+            if s in (3, 11):
+                broadcast(s // 8 + 1, 1)
+            if s == 1:
+                load_pw(2)
+            if s >= 4 and s % 4 == 0 and s // 4 + 2 < 2 * NB:
+                load_pw(s // 4 + 2)
+        make_rstd(N_SLOTS - 1)
+        finish(N_SLOTS - 1)

@@ -22,9 +22,8 @@ FLOPS = 2 * NB * D * D * D
 N_SLOTS = 8 * NB
 N_UNITS = 8 * NB
 HEAD_UNITS = 6
-C_AHEAD = 2
-PE_C_SLOTS = tuple(range(11, 24))
-V_COPY_UNITS = (19, 21, 23)
+PE_C_SLOTS = tuple(range(0, 13))
+V_COPY_UNITS = tuple(range(6, 20))
 PINNED = True
 
 
@@ -52,12 +51,14 @@ def tile_moietransformerblock_pb_kernel(tc, in_proto, pt_w, pln_g, pln_b, proto_
         grpp = ctx.enter_context(tc.tile_pool(name="grpp", bufs=4))
         codep = ctx.enter_context(tc.tile_pool(name="codep", bufs=2))
         xsp = ctx.enter_context(tc.tile_pool(name="xsp", bufs=3))
-        tpool = ctx.enter_context(tc.tile_pool(name="tpool", bufs=4))
-        cpool = ctx.enter_context(tc.tile_pool(name="cpool", bufs=4))
+        tpool = ctx.enter_context(tc.tile_pool(name="tpool", bufs=5))
+        capool = ctx.enter_context(tc.tile_pool(name="capool", bufs=3))
+        cbpool = ctx.enter_context(tc.tile_pool(name="cbpool", bufs=2))
         smallp = ctx.enter_context(tc.tile_pool(name="smallp", bufs=4))
         psum_t = ctx.enter_context(tc.psum_pool(name="psum_t", bufs=2))
         psum_c = ctx.enter_context(tc.psum_pool(name="psum_c", bufs=2))
-        psum_x = ctx.enter_context(tc.psum_pool(name="psum_x", bufs=4))
+        psum_x = ctx.enter_context(tc.psum_pool(name="psum_x", bufs=2))
+        psum_g = ctx.enter_context(tc.psum_pool(name="psum_g", bufs=2))
 
         stage = const.tile([1, 2 * NB * D], BF16, name="stage")
         nc.scalar.dma_start(out=stage[0:1, 0 : NB * D], in_=pln_g.rearrange("(o n) d -> o (n d)", o=1))
@@ -76,7 +77,6 @@ def tile_moietransformerblock_pb_kernel(tc, in_proto, pt_w, pln_g, pln_b, proto_
         bpad = const.tile([P, NB * D], BF16, name="bpad")
         nc.vector.memset(gpad[:].bitcast(I32), 0)
         nc.vector.memset(bpad[:].bitcast(I32), 0)
-        g_all = const.tile([P, NB * D], BF16, name="g_all")
         b_all = const.tile([P, NB * D], BF16, name="b_all")
         junk = const.tile([P, D], BF16, name="junk")
         junk2 = const.tile([P, 2], F32, name="junk2")
@@ -84,7 +84,8 @@ def tile_moietransformerblock_pb_kernel(tc, in_proto, pt_w, pln_g, pln_b, proto_
         raw = {}
         pw_raw = {}
         codes = {}
-        c_tiles = {}
+        ca_tiles = {}
+        cb_tiles = {}
         state = {}
 
         def load_chunk(c):
@@ -107,16 +108,21 @@ def tile_moietransformerblock_pb_kernel(tc, in_proto, pt_w, pln_g, pln_b, proto_
             )
             pw_raw[k] = t_pw
 
-        def broadcast(n, which):
-            src, dst = ((gpad, g_all), (bpad, b_all))[which]
+        def broadcast_b(n):
             for h in range(2):
                 cols = slice(n * D + H * h, n * D + H * h + H)
                 ps = psum_t.tile([P, H], F32, name="bc", tag="tr")
-                nc.tensor.matmul(ps[:], lhsT=ones[:], rhs=src[:, cols], start=True, stop=True)
-                if h == 0:
-                    nc.scalar.copy(out=dst[:, cols], in_=ps[:])
-                else:
-                    nc.vector.tensor_copy(out=dst[:, cols], in_=ps[:])
+                nc.tensor.matmul(ps[:], lhsT=ones[:], rhs=bpad[:, cols], start=True, stop=True)
+                nc.scalar.copy(out=b_all[:, cols], in_=ps[:])
+
+        def broadcast_g(n):
+            tiles = []
+            for h in range(2):
+                cols = slice(n * D + H * h, n * D + H * h + H)
+                g_h = psum_g.tile([P, H], F32, name="gps", tag="gps")
+                nc.tensor.matmul(g_h[:], lhsT=ones[:], rhs=gpad[:, cols], start=True, stop=True)
+                tiles.append(g_h)
+            return tiles
 
         def unit_front(u):
             c, g = divmod(u, 2)
@@ -152,18 +158,23 @@ def tile_moietransformerblock_pb_kernel(tc, in_proto, pt_w, pln_g, pln_b, proto_
             cols = slice(H * j, H * j + H)
             nc.vector.quantize_mx(out=cd[:, g, cols].bitcast(FP8X4), scales=sc[:, g, cols], in_=grp[:])
 
-        def make_c(s):
+        def make_ca(s):
             n = s // 8
             k, tl = divmod(s, 4)
-            c_t = cpool.tile([P, D], F32, name="c%d" % s, tag="c")
-            lo = H if s in PE_C_SLOTS else 0
+            c_t = capool.tile([P, H], F32, name="ca%d" % s, tag="ca")
             nc.vector.tensor_tensor(
-                out=c_t[:, lo:D],
-                in0=pw_raw[k][:, tl * D + lo : (tl + 1) * D],
-                in1=b_all[:, n * D + lo : (n + 1) * D],
-                op=ALU.add,
+                out=c_t[:], in0=pw_raw[k][:, tl * D : tl * D + H], in1=b_all[:, n * D : n * D + H], op=ALU.add
             )
-            c_tiles[s] = c_t
+            ca_tiles[s] = c_t
+
+        def make_cb(s):
+            n = s // 8
+            k, tl = divmod(s, 4)
+            c_t = cbpool.tile([P, H], F32, name="cb%d" % s, tag="cb")
+            nc.gpsimd.tensor_tensor(
+                out=c_t[:], in0=pw_raw[k][:, tl * D + H : (tl + 1) * D], in1=b_all[:, n * D + H : (n + 1) * D], op=ALU.add
+            )
+            cb_tiles[s] = c_t
 
         def make_c_pe(s):
             n = s // 8
@@ -173,20 +184,19 @@ def tile_moietransformerblock_pb_kernel(tc, in_proto, pt_w, pln_g, pln_b, proto_
             nc.tensor.matmul(c_ps[:], lhsT=ones[:], rhs=bpad[:, n * D : n * D + H], start=False, stop=True)
             return c_ps
 
-        def finish(s):
+        def finish_b(s):
+            t_t, rstd, c_ps = state[s]
+            nc.vector.scalar_tensor_tensor(
+                out=t_t[:, H:D], in0=t_t[:, H:D], scalar=rstd[:], in1=cb_tiles[s][:], op0=ALU.mult, op1=ALU.add
+            )
+
+        def finish_a(s):
             n, i = divmod(s, 8)
             t_t, rstd, c_ps = state[s]
-            if c_ps is not None:
-                nc.vector.scalar_tensor_tensor(
-                    out=t_t[:, 0:H], in0=t_t[:, 0:H], scalar=rstd[:], in1=c_ps[:], op0=ALU.mult, op1=ALU.add
-                )
-                nc.vector.scalar_tensor_tensor(
-                    out=t_t[:, H:D], in0=t_t[:, H:D], scalar=rstd[:], in1=c_tiles[s][:, H:D], op0=ALU.mult, op1=ALU.add
-                )
-            else:
-                nc.vector.scalar_tensor_tensor(
-                    out=t_t[:], in0=t_t[:], scalar=rstd[:], in1=c_tiles[s][:], op0=ALU.mult, op1=ALU.add
-                )
+            c_a = c_ps if c_ps is not None else ca_tiles[s]
+            nc.vector.scalar_tensor_tensor(
+                out=t_t[:, 0:H], in0=t_t[:, 0:H], scalar=rstd[:], in1=c_a[:], op0=ALU.mult, op1=ALU.add
+            )
             nc.sync.dma_start(out=out_view[n][:, i, :], in_=t_t[:])
 
         def make_rstd(s):
@@ -210,12 +220,14 @@ def tile_moietransformerblock_pb_kernel(tc, in_proto, pt_w, pln_g, pln_b, proto_
                 nc.vector.tensor_copy(out=gpad[0:1, :], in_=stage[0:1, 0 : NB * D])
                 nc.vector.tensor_copy(out=bpad[0:1, :], in_=stage[0:1, NB * D : 2 * NB * D])
             if u == 3:
-                broadcast(0, 0)
-                broadcast(0, 1)
+                g_ps = broadcast_g(0)
+                broadcast_b(0)
                 load_pw(1)
         unit_back(pending)
-        for s in range(C_AHEAD):
-            make_c(s)
+        make_cb(0)
+        if 0 not in PE_C_SLOTS:
+            make_ca(0)
+        waiting = []
 
         for s in range(N_SLOTS):
             n, i = divmod(s, 8)
@@ -244,29 +256,36 @@ def tile_moietransformerblock_pb_kernel(tc, in_proto, pt_w, pln_g, pln_b, proto_
                 make_rstd(s - 1)
             nc.scalar.activation(out=xs[:, H:D], in_=x_ps[1][:], func=ACT.Copy, accum_out=sums[:, 1:2])
             if s > 0:
-                finish(s - 1)
-            if s + C_AHEAD < N_SLOTS:
-                make_c(s + C_AHEAD)
+                finish_b(s - 1)
+            for info in waiting:
+                unit_back(info)
+            if s + 1 < N_SLOTS:
+                make_cb(s + 1)
+                if s + 1 not in PE_C_SLOTS:
+                    make_ca(s + 1)
+            if s > 0:
+                finish_a(s - 1)
+            if s > 0 and i == 0:
+                g_ps = broadcast_g(n)
             c_ps = make_c_pe(s) if s in PE_C_SLOTS else None
-            infos = [unit_front(u) for u in units_of_slot(s)]
+            waiting = [unit_front(u) for u in units_of_slot(s)]
             negmean = smallp.tile([P, 1], F32, name="nm%d" % s, tag="nm")
             nc.scalar.activation(out=junk2[:], in_=sums[:], func=ACT.Copy, scale=-1.0 / D, accum_out=negmean[:])
             t_t = tpool.tile([P, D], F32, name="t%d" % s, tag="t")
-            nc.vector.scalar_tensor_tensor(
-                out=t_t[:], in0=xs[:], scalar=negmean[:], in1=g_all[:, n * D : (n + 1) * D], op0=ALU.add, op1=ALU.mult
-            )
+            for h in range(2):
+                cols = slice(H * h, H * h + H)
+                nc.vector.scalar_tensor_tensor(
+                    out=t_t[:, cols], in0=xs[:, cols], scalar=negmean[:], in1=g_ps[h][:], op0=ALU.add, op1=ALU.mult
+                )
             ssq = smallp.tile([P, 1], F32, name="ssq%d" % s, tag="ssq")
             nc.scalar.activation(out=junk[:], in_=xs[:], func=ACT.Square, bias=negmean[:], scale=1.0, accum_out=ssq[:])
             state[s] = (t_t, ssq, c_ps)
-            for info in infos:
-                unit_back(info)
             if s in (2, 10):
-                broadcast(s // 8 + 1, 0)
-            if s in (3, 11):
-                broadcast(s // 8 + 1, 1)
+                broadcast_b(s // 8 + 1)
             if s == 1:
                 load_pw(2)
             if s >= 4 and s % 4 == 0 and s // 4 + 2 < 2 * NB:
                 load_pw(s // 4 + 2)
         make_rstd(N_SLOTS - 1)
-        finish(N_SLOTS - 1)
+        finish_b(N_SLOTS - 1)
+        finish_a(N_SLOTS - 1)

@@ -22,16 +22,14 @@ FLOPS = 2 * NB * D * D * D
 N_SLOTS = 8 * NB
 N_UNITS = 8 * NB
 HEAD_UNITS = 6
-PE_C_SLOTS = tuple(range(0, 13))
-V_COPY_UNITS = tuple(range(6, 20))
-PINNED = True
+PE_C_SLOTS = tuple(range(4, 17))
+EARLY_C_SLOTS = (0, 1, 2, 3)
+B_SLOTS = {2: (1, 1), 3: (1, 0), 10: (2, 1), 11: (2, 0)}
 
 
 def units_of_slot(s):
     if s == 0:
-        return [6]
-    if s == 1:
-        return [7, 8]
+        return [6, 7]
     return [s + 7] if s + 7 < N_UNITS else []
 
 
@@ -43,8 +41,7 @@ def tile_moietransformerblock_pb_kernel(tc, in_proto, pt_w, pln_g, pln_b, proto_
     out_view = out.rearrange("n (p t) d -> n p t d", t=8)
 
     with ExitStack() as ctx:
-        if PINNED:
-            ctx.enter_context(tc.manual_schedule())
+        ctx.enter_context(tc.manual_schedule())
         const = ctx.enter_context(tc.tile_pool(name="const", bufs=1))
         rawp = ctx.enter_context(tc.tile_pool(name="rawp", bufs=4))
         pwp = ctx.enter_context(tc.tile_pool(name="pwp", bufs=3))
@@ -52,13 +49,14 @@ def tile_moietransformerblock_pb_kernel(tc, in_proto, pt_w, pln_g, pln_b, proto_
         codep = ctx.enter_context(tc.tile_pool(name="codep", bufs=2))
         xsp = ctx.enter_context(tc.tile_pool(name="xsp", bufs=3))
         tpool = ctx.enter_context(tc.tile_pool(name="tpool", bufs=5))
-        capool = ctx.enter_context(tc.tile_pool(name="capool", bufs=3))
+        capool = ctx.enter_context(tc.tile_pool(name="capool", bufs=5))
         cbpool = ctx.enter_context(tc.tile_pool(name="cbpool", bufs=2))
         smallp = ctx.enter_context(tc.tile_pool(name="smallp", bufs=4))
         psum_t = ctx.enter_context(tc.psum_pool(name="psum_t", bufs=2))
         psum_c = ctx.enter_context(tc.psum_pool(name="psum_c", bufs=2))
         psum_x = ctx.enter_context(tc.psum_pool(name="psum_x", bufs=2))
         psum_g = ctx.enter_context(tc.psum_pool(name="psum_g", bufs=2))
+        tr_homes = ((psum_t, "tr"), (psum_x, "x"), (psum_c, "cps"))
 
         stage = const.tile([1, 2 * NB * D], BF16, name="stage")
         nc.scalar.dma_start(out=stage[0:1, 0 : NB * D], in_=pln_g.rearrange("(o n) d -> o (n d)", o=1))
@@ -77,6 +75,8 @@ def tile_moietransformerblock_pb_kernel(tc, in_proto, pt_w, pln_g, pln_b, proto_
         bpad = const.tile([P, NB * D], BF16, name="bpad")
         nc.vector.memset(gpad[:].bitcast(I32), 0)
         nc.vector.memset(bpad[:].bitcast(I32), 0)
+        nc.vector.tensor_copy(out=gpad[0:1, :], in_=stage[0:1, 0 : NB * D])
+        nc.vector.tensor_copy(out=bpad[0:1, :], in_=stage[0:1, NB * D : 2 * NB * D])
         b_all = const.tile([P, NB * D], BF16, name="b_all")
         junk = const.tile([P, D], BF16, name="junk")
         junk2 = const.tile([P, 2], F32, name="junk2")
@@ -86,7 +86,9 @@ def tile_moietransformerblock_pb_kernel(tc, in_proto, pt_w, pln_g, pln_b, proto_
         codes = {}
         ca_tiles = {}
         cb_tiles = {}
+        cps_tiles = {}
         state = {}
+        unit = {}
 
         def load_chunk(c):
             n, r = divmod(c, 4)
@@ -108,12 +110,11 @@ def tile_moietransformerblock_pb_kernel(tc, in_proto, pt_w, pln_g, pln_b, proto_
             )
             pw_raw[k] = t_pw
 
-        def broadcast_b(n):
-            for h in range(2):
-                cols = slice(n * D + H * h, n * D + H * h + H)
-                ps = psum_t.tile([P, H], F32, name="bc", tag="tr")
-                nc.tensor.matmul(ps[:], lhsT=ones[:], rhs=bpad[:, cols], start=True, stop=True)
-                nc.scalar.copy(out=b_all[:, cols], in_=ps[:])
+        def broadcast_b(n, h):
+            cols = slice(n * D + H * h, n * D + H * h + H)
+            ps = psum_t.tile([P, H], F32, name="bc", tag="tr")
+            nc.tensor.matmul(ps[:], lhsT=ones[:], rhs=bpad[:, cols], start=True, stop=True)
+            nc.scalar.copy(out=b_all[:, cols], in_=ps[:])
 
         def broadcast_g(n):
             tiles = []
@@ -124,7 +125,7 @@ def tile_moietransformerblock_pb_kernel(tc, in_proto, pt_w, pln_g, pln_b, proto_
                 tiles.append(g_h)
             return tiles
 
-        def unit_front(u):
+        def unit_front(u, home):
             c, g = divmod(u, 2)
             n, r = divmod(c, 4)
             op = 0 if r < 2 else 1
@@ -133,27 +134,28 @@ def tile_moietransformerblock_pb_kernel(tc, in_proto, pt_w, pln_g, pln_b, proto_
                 cd = codep.tile([P, 2, D], U32, name="cd%d_%d" % (n, op), tag="cd%d" % op, align_bytes=64)
                 sc = codep.tile([P, 2, D], U8, name="sc%d_%d" % (n, op), tag="sc%d" % op, align_bytes=64)
                 codes[(n, op)] = (cd, sc)
+            pool, tag = tr_homes[home]
             words = raw[c][:].bitcast(F32)
             grp = grpp.tile([P, 2048], BF16, name="grp%d" % u, tag="grp", align_bytes=64)
             grp_w = grp[:].bitcast(F32).rearrange("p (a r w) -> p a r w", a=4, w=2)
             for h in range(2):
-                ps = psum_t.tile([P, 2, 2, P], F32, name="tr", tag="tr")
+                ps = pool.tile([P, 2, 2, P], F32, name="tr", tag=tag)
                 for tl in range(2):
                     for w in range(2):
                         col = H * (2 * h + tl) + 256 * g + P * w
                         nc.tensor.transpose(ps[:, tl, w, :], words[:, col : col + P], ident[:])
                 src = ps[:].rearrange("p a w r -> p a r w")
                 dst = grp_w[:, 2 * h : 2 * h + 2]
-                if h == 1 and (u < HEAD_UNITS or u in V_COPY_UNITS):
+                if h == 1:
                     nc.vector.tensor_copy(out=dst, in_=src)
                 else:
                     nc.scalar.copy(out=dst, in_=src)
             if g == 1 and c + 4 < 4 * NB:
                 load_chunk(c + 4)
-            return (n, op, g, j, grp)
+            unit[u] = (n, op, g, j, grp)
 
-        def unit_back(info):
-            n, op, g, j, grp = info
+        def unit_back(u):
+            n, op, g, j, grp = unit[u]
             cd, sc = codes[(n, op)]
             cols = slice(H * j, H * j + H)
             nc.vector.quantize_mx(out=cd[:, g, cols].bitcast(FP8X4), scales=sc[:, g, cols], in_=grp[:])
@@ -182,51 +184,46 @@ def tile_moietransformerblock_pb_kernel(tc, in_proto, pt_w, pln_g, pln_b, proto_
             c_ps = psum_c.tile([P, H], F32, name="cps", tag="cps")
             nc.tensor.matmul(c_ps[:], lhsT=identb[:], rhs=pw_raw[k][:, tl * D : tl * D + H], start=True, stop=False)
             nc.tensor.matmul(c_ps[:], lhsT=ones[:], rhs=bpad[:, n * D : n * D + H], start=False, stop=True)
-            return c_ps
+            cps_tiles[s] = c_ps
 
         def finish_b(s):
-            t_t, rstd, c_ps = state[s]
+            t_t, rstd = state[s]
             nc.vector.scalar_tensor_tensor(
                 out=t_t[:, H:D], in0=t_t[:, H:D], scalar=rstd[:], in1=cb_tiles[s][:], op0=ALU.mult, op1=ALU.add
             )
 
         def finish_a(s):
             n, i = divmod(s, 8)
-            t_t, rstd, c_ps = state[s]
-            c_a = c_ps if c_ps is not None else ca_tiles[s]
+            t_t, rstd = state[s]
+            c_a = cps_tiles[s] if s in PE_C_SLOTS else ca_tiles[s]
             nc.vector.scalar_tensor_tensor(
                 out=t_t[:, 0:H], in0=t_t[:, 0:H], scalar=rstd[:], in1=c_a[:], op0=ALU.mult, op1=ALU.add
             )
             nc.sync.dma_start(out=out_view[n][:, i, :], in_=t_t[:])
 
         def make_rstd(s):
-            t_t, ssq, c_ps = state[s]
+            t_t, ssq = state[s]
             rstd = smallp.tile([P, 1], F32, name="rstd%d" % s, tag="rstd")
             nc.scalar.activation(out=rstd[:], in_=ssq[:], func=ACT.Abs_reciprocal_sqrt, bias=eps[:], scale=1.0 / D)
-            state[s] = (t_t, rstd, c_ps)
+            state[s] = (t_t, rstd)
 
         load_chunk(0)
         load_chunk(1)
         load_chunk(2)
         load_pw(0)
         load_chunk(3)
-        pending = None
         for u in range(HEAD_UNITS):
-            info = unit_front(u)
-            if pending is not None:
-                unit_back(pending)
-            pending = info
-            if u == 1:
-                nc.vector.tensor_copy(out=gpad[0:1, :], in_=stage[0:1, 0 : NB * D])
-                nc.vector.tensor_copy(out=bpad[0:1, :], in_=stage[0:1, NB * D : 2 * NB * D])
+            unit_front(u, u % 3)
+            if 0 < u < HEAD_UNITS - 1:
+                unit_back(u - 1)
+            if u >= HEAD_UNITS - 2:
+                unit_back(u)
             if u == 3:
-                g_ps = broadcast_g(0)
-                broadcast_b(0)
                 load_pw(1)
-        unit_back(pending)
+        g_ps = broadcast_g(0)
+        broadcast_b(0, 1)
+        broadcast_b(0, 0)
         make_cb(0)
-        if 0 not in PE_C_SLOTS:
-            make_ca(0)
         waiting = []
 
         for s in range(N_SLOTS):
@@ -251,37 +248,43 @@ def tile_moietransformerblock_pb_kernel(tc, in_proto, pt_w, pln_g, pln_b, proto_
                         stop=(g == 1),
                     )
                 x_ps.append(x_h)
+            if s == 0:
+                for e in EARLY_C_SLOTS:
+                    make_ca(e)
             nc.scalar.activation(out=xs[:, 0:H], in_=x_ps[0][:], func=ACT.Copy, accum_out=sums[:, 0:1])
             if s > 0:
                 make_rstd(s - 1)
             nc.scalar.activation(out=xs[:, H:D], in_=x_ps[1][:], func=ACT.Copy, accum_out=sums[:, 1:2])
             if s > 0:
                 finish_b(s - 1)
-            for info in waiting:
-                unit_back(info)
+            for u in waiting:
+                unit_back(u)
             if s + 1 < N_SLOTS:
                 make_cb(s + 1)
-                if s + 1 not in PE_C_SLOTS:
+                if s + 1 not in PE_C_SLOTS and s + 1 not in EARLY_C_SLOTS:
                     make_ca(s + 1)
             if s > 0:
+                if s - 1 in PE_C_SLOTS:
+                    make_c_pe(s - 1)
                 finish_a(s - 1)
+            waiting = units_of_slot(s)
+            for k, u in enumerate(waiting):
+                unit_front(u, 2 * k)
             if s > 0 and i == 0:
                 g_ps = broadcast_g(n)
-            c_ps = make_c_pe(s) if s in PE_C_SLOTS else None
-            waiting = [unit_front(u) for u in units_of_slot(s)]
             negmean = smallp.tile([P, 1], F32, name="nm%d" % s, tag="nm")
             nc.scalar.activation(out=junk2[:], in_=sums[:], func=ACT.Copy, scale=-1.0 / D, accum_out=negmean[:])
             t_t = tpool.tile([P, D], F32, name="t%d" % s, tag="t")
-            for h in range(2):
+            for h in (1, 0):
                 cols = slice(H * h, H * h + H)
                 nc.vector.scalar_tensor_tensor(
                     out=t_t[:, cols], in0=xs[:, cols], scalar=negmean[:], in1=g_ps[h][:], op0=ALU.add, op1=ALU.mult
                 )
             ssq = smallp.tile([P, 1], F32, name="ssq%d" % s, tag="ssq")
             nc.scalar.activation(out=junk[:], in_=xs[:], func=ACT.Square, bias=negmean[:], scale=1.0, accum_out=ssq[:])
-            state[s] = (t_t, ssq, c_ps)
-            if s in (2, 10):
-                broadcast_b(s // 8 + 1)
+            state[s] = (t_t, ssq)
+            if s in B_SLOTS:
+                broadcast_b(B_SLOTS[s][0], B_SLOTS[s][1])
             if s == 1:
                 load_pw(2)
             if s >= 4 and s % 4 == 0 and s // 4 + 2 < 2 * NB:

@@ -22,7 +22,7 @@ FLOPS = 2 * NB * D * D * D
 N_SLOTS = 8 * NB
 N_UNITS = 8 * NB
 HEAD_UNITS = 6
-PE_C_SLOTS = tuple(range(4, 17))
+PE_C_SLOTS = tuple(range(4, 23))
 EARLY_C_SLOTS = (0, 1, 2, 3)
 B_SLOTS = {2: (1, 1), 3: (1, 0), 10: (2, 1), 11: (2, 0)}
 
@@ -58,9 +58,9 @@ def tile_moietransformerblock_pb_kernel(tc, in_proto, pt_w, pln_g, pln_b, proto_
         psum_g = ctx.enter_context(tc.psum_pool(name="psum_g", bufs=2))
         tr_homes = ((psum_t, "tr"), (psum_x, "x"), (psum_c, "cps"))
 
-        stage = const.tile([1, 2 * NB * D], BF16, name="stage")
-        nc.scalar.dma_start(out=stage[0:1, 0 : NB * D], in_=pln_g.rearrange("(o n) d -> o (n d)", o=1))
-        nc.scalar.dma_start(out=stage[0:1, NB * D : 2 * NB * D], in_=pln_b.rearrange("(o n) d -> o (n d)", o=1))
+        gb_stage = const.tile([2 * NB * 8, P], BF16, name="gb_stage")
+        nc.scalar.dma_start(out=gb_stage[0 : NB * 8, :], in_=pln_g.rearrange("n (q c) -> (n q) c", c=P))
+        nc.scalar.dma_start(out=gb_stage[NB * 8 : 2 * NB * 8, :], in_=pln_b.rearrange("n (q c) -> (n q) c", c=P))
         ident = const.tile([P, P], F32, name="ident")
         make_identity(nc, ident[:])
         identb = const.tile([P, P], BF16, name="identb")
@@ -69,14 +69,16 @@ def tile_moietransformerblock_pb_kernel(tc, in_proto, pt_w, pln_g, pln_b, proto_
         nc.vector.memset(eps[:], LN_EPS)
         warm = const.tile([P, 1], F32, name="warm")
         nc.scalar.activation(out=warm[:], in_=eps[:], func=ACT.Abs_reciprocal_sqrt, bias=eps[:], scale=1.0)
-        ones = const.tile([P, P], BF16, name="ones")
-        nc.vector.memset(ones[:], 1.0)
-        gpad = const.tile([P, NB * D], BF16, name="gpad")
-        bpad = const.tile([P, NB * D], BF16, name="bpad")
-        nc.vector.memset(gpad[:].bitcast(I32), 0)
-        nc.vector.memset(bpad[:].bitcast(I32), 0)
-        nc.vector.tensor_copy(out=gpad[0:1, :], in_=stage[0:1, 0 : NB * D])
-        nc.vector.tensor_copy(out=bpad[0:1, :], in_=stage[0:1, NB * D : 2 * NB * D])
+        row0 = const.tile([P, P], BF16, name="row0")
+        nc.vector.memset(row0[:].bitcast(I32), 0)
+        nc.vector.memset(row0[0:1, :], 1.0)
+        gb_rows = const.tile([P, P], BF16, name="gb_rows")
+        nc.vector.memset(gb_rows[:].bitcast(I32), 0)
+        nc.vector.tensor_copy(out=gb_rows[0 : 2 * NB * 8, :], in_=gb_stage[:])
+        gb_cols = const.tile([P, 2 * NB * 8], F32, name="gb_cols")
+        gb_ps = psum_g.tile([P, P], BF16, name="gb_ps", tag="gps")
+        nc.tensor.transpose(gb_ps[:], gb_rows[:], identb[:])
+        nc.vector.tensor_copy(out=gb_cols[:], in_=gb_ps[:, 0 : 2 * NB * 8])
         b_all = const.tile([P, NB * D], BF16, name="b_all")
         junk = const.tile([P, D], BF16, name="junk")
         junk2 = const.tile([P, 2], F32, name="junk2")
@@ -110,18 +112,23 @@ def tile_moietransformerblock_pb_kernel(tc, in_proto, pt_w, pln_g, pln_b, proto_
             )
             pw_raw[k] = t_pw
 
+        def spread(ps, first):
+            for q in range(4):
+                nc.tensor.transpose(
+                    ps[:, q * P : (q + 1) * P], gb_cols[:, first + q : first + q + 1].to_broadcast([P, P]), ident[:]
+                )
+
         def broadcast_b(n, h):
             cols = slice(n * D + H * h, n * D + H * h + H)
             ps = psum_t.tile([P, H], F32, name="bc", tag="tr")
-            nc.tensor.matmul(ps[:], lhsT=ones[:], rhs=bpad[:, cols], start=True, stop=True)
+            spread(ps, NB * 8 + n * 8 + 4 * h)
             nc.scalar.copy(out=b_all[:, cols], in_=ps[:])
 
         def broadcast_g(n):
             tiles = []
             for h in range(2):
-                cols = slice(n * D + H * h, n * D + H * h + H)
                 g_h = psum_g.tile([P, H], F32, name="gps", tag="gps")
-                nc.tensor.matmul(g_h[:], lhsT=ones[:], rhs=gpad[:, cols], start=True, stop=True)
+                spread(g_h, n * 8 + 4 * h)
                 tiles.append(g_h)
             return tiles
 
@@ -183,7 +190,7 @@ def tile_moietransformerblock_pb_kernel(tc, in_proto, pt_w, pln_g, pln_b, proto_
             k, tl = divmod(s, 4)
             c_ps = psum_c.tile([P, H], F32, name="cps", tag="cps")
             nc.tensor.matmul(c_ps[:], lhsT=identb[:], rhs=pw_raw[k][:, tl * D : tl * D + H], start=True, stop=False)
-            nc.tensor.matmul(c_ps[:], lhsT=ones[:], rhs=bpad[:, n * D : n * D + H], start=False, stop=True)
+            nc.tensor.matmul(c_ps[:], lhsT=row0[:], rhs=b_all[:, n * D : n * D + H], start=False, stop=True)
             cps_tiles[s] = c_ps
 
         def finish_b(s):

@@ -74,11 +74,8 @@ def tile_moietransformerblock_pb_kernel(tc, in_proto, pt_w, pln_g, pln_b, proto_
         nc.vector.memset(row0[0:1, :], 1.0)
         gb_rows = const.tile([P, P], BF16, name="gb_rows")
         nc.vector.memset(gb_rows[:].bitcast(I32), 0)
-        nc.vector.tensor_copy(out=gb_rows[0 : 2 * NB * 8, :], in_=gb_stage[:])
+        nc.gpsimd.tensor_copy(out=gb_rows[0 : 2 * NB * 8, :], in_=gb_stage[:])
         gb_cols = const.tile([P, 2 * NB * 8], F32, name="gb_cols")
-        gb_ps = psum_g.tile([P, P], BF16, name="gb_ps", tag="gps")
-        nc.tensor.transpose(gb_ps[:], gb_rows[:], identb[:])
-        nc.vector.tensor_copy(out=gb_cols[:], in_=gb_ps[:, 0 : 2 * NB * 8])
         b_all = const.tile([P, NB * D], BF16, name="b_all")
         junk = const.tile([P, D], BF16, name="junk")
         junk2 = const.tile([P, 2], F32, name="junk2")
@@ -227,6 +224,9 @@ def tile_moietransformerblock_pb_kernel(tc, in_proto, pt_w, pln_g, pln_b, proto_
                 unit_back(u)
             if u == 3:
                 load_pw(1)
+                gb_ps = psum_g.tile([P, P], BF16, name="gb_ps", tag="gps")
+                nc.tensor.transpose(gb_ps[:], gb_rows[:], identb[:])
+                nc.vector.tensor_copy(out=gb_cols[:], in_=gb_ps[:, 0 : 2 * NB * 8])
         g_ps = broadcast_g(0)
         broadcast_b(0, 1)
         broadcast_b(0, 0)

@@ -22,7 +22,7 @@ FLOPS = 2 * NB * D * D * D
 N_SLOTS = 8 * NB
 N_UNITS = 8 * NB
 HEAD_UNITS = 6
-PE_C_SLOTS = tuple(range(4, 23))
+PE_C_SLOTS = tuple(range(4, 17))
 EARLY_C_SLOTS = (0, 1, 2, 3)
 B_SLOTS = {2: (1, 1), 3: (1, 0), 10: (2, 1), 11: (2, 0)}
 
@@ -58,9 +58,12 @@ def tile_moietransformerblock_pb_kernel(tc, in_proto, pt_w, pln_g, pln_b, proto_
         psum_g = ctx.enter_context(tc.psum_pool(name="psum_g", bufs=2))
         tr_homes = ((psum_t, "tr"), (psum_x, "x"), (psum_c, "cps"))
 
-        gb_stage = const.tile([2 * NB * 8, P], BF16, name="gb_stage")
-        nc.scalar.dma_start(out=gb_stage[0 : NB * 8, :], in_=pln_g.rearrange("n (q c) -> (n q) c", c=P))
-        nc.scalar.dma_start(out=gb_stage[NB * 8 : 2 * NB * 8, :], in_=pln_b.rearrange("n (q c) -> (n q) c", c=P))
+        gpad = const.tile([P, NB * D], BF16, name="gpad")
+        bpad = const.tile([P, NB * D], BF16, name="bpad")
+        nc.vector.memset(gpad[:].bitcast(I32), 0)
+        nc.scalar.dma_start(out=gpad[0:1, :], in_=pln_g.rearrange("(o n) d -> o (n d)", o=1))
+        nc.vector.memset(bpad[:].bitcast(I32), 0)
+        nc.scalar.dma_start(out=bpad[0:1, :], in_=pln_b.rearrange("(o n) d -> o (n d)", o=1))
         ident = const.tile([P, P], F32, name="ident")
         make_identity(nc, ident[:])
         identb = const.tile([P, P], BF16, name="identb")
@@ -69,13 +72,8 @@ def tile_moietransformerblock_pb_kernel(tc, in_proto, pt_w, pln_g, pln_b, proto_
         nc.vector.memset(eps[:], LN_EPS)
         warm = const.tile([P, 1], F32, name="warm")
         nc.scalar.activation(out=warm[:], in_=eps[:], func=ACT.Abs_reciprocal_sqrt, bias=eps[:], scale=1.0)
-        row0 = const.tile([P, P], BF16, name="row0")
-        nc.vector.memset(row0[:].bitcast(I32), 0)
-        nc.vector.memset(row0[0:1, :], 1.0)
-        gb_rows = const.tile([P, P], BF16, name="gb_rows")
-        nc.vector.memset(gb_rows[:].bitcast(I32), 0)
-        nc.gpsimd.tensor_copy(out=gb_rows[0 : 2 * NB * 8, :], in_=gb_stage[:])
-        gb_cols = const.tile([P, 2 * NB * 8], F32, name="gb_cols")
+        ones = const.tile([P, P], BF16, name="ones")
+        nc.vector.memset(ones[:], 1.0)
         b_all = const.tile([P, NB * D], BF16, name="b_all")
         junk = const.tile([P, D], BF16, name="junk")
         junk2 = const.tile([P, 2], F32, name="junk2")
@@ -109,23 +107,18 @@ def tile_moietransformerblock_pb_kernel(tc, in_proto, pt_w, pln_g, pln_b, proto_
             )
             pw_raw[k] = t_pw
 
-        def spread(ps, first):
-            for q in range(4):
-                nc.tensor.transpose(
-                    ps[:, q * P : (q + 1) * P], gb_cols[:, first + q : first + q + 1].to_broadcast([P, P]), ident[:]
-                )
-
         def broadcast_b(n, h):
             cols = slice(n * D + H * h, n * D + H * h + H)
             ps = psum_t.tile([P, H], F32, name="bc", tag="tr")
-            spread(ps, NB * 8 + n * 8 + 4 * h)
+            nc.tensor.matmul(ps[:], lhsT=ones[:], rhs=bpad[:, cols], start=True, stop=True)
             nc.scalar.copy(out=b_all[:, cols], in_=ps[:])
 
         def broadcast_g(n):
             tiles = []
             for h in range(2):
+                cols = slice(n * D + H * h, n * D + H * h + H)
                 g_h = psum_g.tile([P, H], F32, name="gps", tag="gps")
-                spread(g_h, n * 8 + 4 * h)
+                nc.tensor.matmul(g_h[:], lhsT=ones[:], rhs=gpad[:, cols], start=True, stop=True)
                 tiles.append(g_h)
             return tiles
 
@@ -187,7 +180,7 @@ def tile_moietransformerblock_pb_kernel(tc, in_proto, pt_w, pln_g, pln_b, proto_
             k, tl = divmod(s, 4)
             c_ps = psum_c.tile([P, H], F32, name="cps", tag="cps")
             nc.tensor.matmul(c_ps[:], lhsT=identb[:], rhs=pw_raw[k][:, tl * D : tl * D + H], start=True, stop=False)
-            nc.tensor.matmul(c_ps[:], lhsT=row0[:], rhs=b_all[:, n * D : n * D + H], start=False, stop=True)
+            nc.tensor.matmul(c_ps[:], lhsT=ones[:], rhs=bpad[:, n * D : n * D + H], start=False, stop=True)
             cps_tiles[s] = c_ps
 
         def finish_b(s):
@@ -224,9 +217,6 @@ def tile_moietransformerblock_pb_kernel(tc, in_proto, pt_w, pln_g, pln_b, proto_
                 unit_back(u)
             if u == 3:
                 load_pw(1)
-                gb_ps = psum_g.tile([P, P], BF16, name="gb_ps", tag="gps")
-                nc.tensor.transpose(gb_ps[:], gb_rows[:], identb[:])
-                nc.vector.tensor_copy(out=gb_cols[:], in_=gb_ps[:, 0 : 2 * NB * 8])
         g_ps = broadcast_g(0)
         broadcast_b(0, 1)
         broadcast_b(0, 0)

from contextlib import ExitStack

import concourse.mybir as mybir
from concourse.masks import make_identity

F32 = mybir.dt.float32
BF16 = mybir.dt.bfloat16
U32 = mybir.dt.uint32
U8 = mybir.dt.uint8
I32 = mybir.dt.int32
FP8X4 = mybir.dt.float8_e4m3fn_x4
ACT = mybir.ActivationFunctionType
ALU = mybir.AluOpType

NB = 3
D = 1024
P = 128
H = 512
LN_EPS = 1e-5
FLOPS = 2 * NB * D * D * D

N_SLOTS = 8 * NB
N_UNITS = 8 * NB
HEAD_UNITS = 6
PE_C_SLOTS = tuple(range(4, 17))
EARLY_C_SLOTS = (0, 1, 2, 3)
B_SLOTS = {2: (1, 1), 3: (1, 0), 10: (2, 1), 11: (2, 0)}


def units_of_slot(s):
    if s == 0:
        return [6, 7]
    return [s + 7] if s + 7 < N_UNITS else []


def tile_moietransformerblock_pb_kernel(tc, in_proto, pt_w, pln_g, pln_b, proto_w, out):
    nc = tc.nc
    a_view = in_proto.rearrange("n (p t) k -> n p t k", t=8)
    w_view = pt_w.rearrange("n (t p) k -> n p t k", p=P)
    pw_view = proto_w.rearrange("n (p t) d -> n p t d", t=8)
    out_view = out.rearrange("n (p t) d -> n p t d", t=8)

    with ExitStack() as ctx:
        ctx.enter_context(tc.manual_schedule())
        const = ctx.enter_context(tc.tile_pool(name="const", bufs=1))
        rawp = ctx.enter_context(tc.tile_pool(name="rawp", bufs=4))
        pwp = ctx.enter_context(tc.tile_pool(name="pwp", bufs=3))
        grpp = ctx.enter_context(tc.tile_pool(name="grpp", bufs=4))
        codep = ctx.enter_context(tc.tile_pool(name="codep", bufs=2))
        xsp = ctx.enter_context(tc.tile_pool(name="xsp", bufs=3))
        tpool = ctx.enter_context(tc.tile_pool(name="tpool", bufs=5))
        capool = ctx.enter_context(tc.tile_pool(name="capool", bufs=5))
        cbpool = ctx.enter_context(tc.tile_pool(name="cbpool", bufs=2))
        smallp = ctx.enter_context(tc.tile_pool(name="smallp", bufs=4))
        psum_t = ctx.enter_context(tc.psum_pool(name="psum_t", bufs=2))
        psum_c = ctx.enter_context(tc.psum_pool(name="psum_c", bufs=2))
        psum_x = ctx.enter_context(tc.psum_pool(name="psum_x", bufs=2))
        psum_g = ctx.enter_context(tc.psum_pool(name="psum_g", bufs=2))
        tr_homes = ((psum_t, "tr"), (psum_x, "x"), (psum_c, "cps"))

        gpad = const.tile([P, NB * D], BF16, name="gpad")
        bpad = const.tile([P, NB * D], BF16, name="bpad")
        nc.vector.memset(gpad[:].bitcast(I32), 0)
        nc.scalar.dma_start(out=gpad[0:1, :], in_=pln_g.rearrange("(o n) d -> o (n d)", o=1))
        nc.vector.memset(bpad[:].bitcast(I32), 0)
        nc.scalar.dma_start(out=bpad[0:1, :], in_=pln_b.rearrange("(o n) d -> o (n d)", o=1))
        ident = const.tile([P, P], F32, name="ident")
        make_identity(nc, ident[:])
        identb = const.tile([P, P], BF16, name="identb")
        make_identity(nc, identb[:])
        eps = const.tile([P, 1], F32, name="eps")
        nc.vector.memset(eps[:], LN_EPS)
        warm = const.tile([P, 1], F32, name="warm")
        nc.scalar.activation(out=warm[:], in_=eps[:], func=ACT.Abs_reciprocal_sqrt, bias=eps[:], scale=1.0)
        ones = const.tile([P, P], BF16, name="ones")
        nc.vector.memset(ones[:], 1.0)
        b_all = const.tile([P, NB * D], BF16, name="b_all")
        junk = const.tile([P, D], BF16, name="junk")
        junk2 = const.tile([P, 2], F32, name="junk2")

        raw = {}
        pw_raw = {}
        codes = {}
        ca_tiles = {}
        cb_tiles = {}
        cps_tiles = {}
        state = {}
        unit = {}

        def load_chunk(c):
            n, r = divmod(c, 4)
            view = w_view if r < 2 else a_view
            j = r % 2
            t_raw = rawp.tile([P, 4 * D], BF16, name="raw%d" % c, tag="raw")
            nc.sync.dma_start(
                out=t_raw[:].rearrange("p (t k) -> p t k", t=4),
                in_=view[n][:, 4 * j : 4 * j + 4, :],
            )
            raw[c] = t_raw

        def load_pw(k):
            n, j = divmod(k, 2)
            t_pw = pwp.tile([P, 4 * D], BF16, name="pw%d" % k, tag="pw")
            nc.sync.dma_start(
                out=t_pw[:].rearrange("p (t k) -> p t k", t=4),
                in_=pw_view[n][:, 4 * j : 4 * j + 4, :],
            )
            pw_raw[k] = t_pw

        def broadcast_b(n, h):
            cols = slice(n * D + H * h, n * D + H * h + H)
            ps = psum_t.tile([P, H], F32, name="bc", tag="tr")
            nc.tensor.matmul(ps[:], lhsT=ones[:], rhs=bpad[:, cols], start=True, stop=True)
            nc.scalar.copy(out=b_all[:, cols], in_=ps[:])

        def broadcast_g(n):
            tiles = []
            for h in range(2):
                cols = slice(n * D + H * h, n * D + H * h + H)
                g_h = psum_g.tile([P, H], F32, name="gps", tag="gps")
                nc.tensor.matmul(g_h[:], lhsT=ones[:], rhs=gpad[:, cols], start=True, stop=True)
                tiles.append(g_h)
            return tiles

        def unit_front(u, home):
            c, g = divmod(u, 2)
            n, r = divmod(c, 4)
            op = 0 if r < 2 else 1
            j = r % 2
            if (n, op) not in codes:
                cd = codep.tile([P, 2, D], U32, name="cd%d_%d" % (n, op), tag="cd%d" % op, align_bytes=64)
                sc = codep.tile([P, 2, D], U8, name="sc%d_%d" % (n, op), tag="sc%d" % op, align_bytes=64)
                codes[(n, op)] = (cd, sc)
            pool, tag = tr_homes[home]
            words = raw[c][:].bitcast(F32)
            grp = grpp.tile([P, 2048], BF16, name="grp%d" % u, tag="grp", align_bytes=64)
            grp_w = grp[:].bitcast(F32).rearrange("p (a r w) -> p a r w", a=4, w=2)
            for h in range(2):
                ps = pool.tile([P, 2, 2, P], F32, name="tr", tag=tag)
                for tl in range(2):
                    for w in range(2):
                        col = H * (2 * h + tl) + 256 * g + P * w
                        nc.tensor.transpose(ps[:, tl, w, :], words[:, col : col + P], ident[:])
                src = ps[:].rearrange("p a w r -> p a r w")
                dst = grp_w[:, 2 * h : 2 * h + 2]
                if h == 1:
                    nc.vector.tensor_copy(out=dst, in_=src)
                else:
                    nc.scalar.copy(out=dst, in_=src)
            if g == 1 and c + 4 < 4 * NB:
                load_chunk(c + 4)
            unit[u] = (n, op, g, j, grp)

        def unit_back(u):
            n, op, g, j, grp = unit[u]
            cd, sc = codes[(n, op)]
            cols = slice(H * j, H * j + H)
            nc.vector.quantize_mx(out=cd[:, g, cols].bitcast(FP8X4), scales=sc[:, g, cols], in_=grp[:])

        def make_ca(s):
            n = s // 8
            k, tl = divmod(s, 4)
            c_t = capool.tile([P, H], F32, name="ca%d" % s, tag="ca")
            nc.vector.tensor_tensor(
                out=c_t[:], in0=pw_raw[k][:, tl * D : tl * D + H], in1=b_all[:, n * D : n * D + H], op=ALU.add
            )
            ca_tiles[s] = c_t

        def make_cb(s):
            n = s // 8
            k, tl = divmod(s, 4)
            c_t = cbpool.tile([P, H], F32, name="cb%d" % s, tag="cb")
            nc.gpsimd.tensor_tensor(
                out=c_t[:], in0=pw_raw[k][:, tl * D + H : (tl + 1) * D], in1=b_all[:, n * D + H : (n + 1) * D], op=ALU.add
            )
            cb_tiles[s] = c_t

        def make_c_pe(s):
            n = s // 8
            k, tl = divmod(s, 4)
            c_ps = psum_c.tile([P, H], F32, name="cps", tag="cps")
            nc.tensor.matmul(c_ps[:], lhsT=identb[:], rhs=pw_raw[k][:, tl * D : tl * D + H], start=True, stop=False)
            nc.tensor.matmul(c_ps[:], lhsT=ones[:], rhs=bpad[:, n * D : n * D + H], start=False, stop=True)
            cps_tiles[s] = c_ps

        def finish_b(s):
            t_t, rstd = state[s]
            nc.vector.scalar_tensor_tensor(
                out=t_t[:, H:D], in0=t_t[:, H:D], scalar=rstd[:], in1=cb_tiles[s][:], op0=ALU.mult, op1=ALU.add
            )

        def finish_a(s):
            n, i = divmod(s, 8)
            t_t, rstd = state[s]
            c_a = cps_tiles[s] if s in PE_C_SLOTS else ca_tiles[s]
            nc.vector.scalar_tensor_tensor(
                out=t_t[:, 0:H], in0=t_t[:, 0:H], scalar=rstd[:], in1=c_a[:], op0=ALU.mult, op1=ALU.add
            )
            nc.sync.dma_start(out=out_view[n][:, i, :], in_=t_t[:])

        def make_rstd(s):
            t_t, ssq = state[s]
            rstd = smallp.tile([P, 1], F32, name="rstd%d" % s, tag="rstd")
            nc.scalar.activation(out=rstd[:], in_=ssq[:], func=ACT.Abs_reciprocal_sqrt, bias=eps[:], scale=1.0 / D)
            state[s] = (t_t, rstd)

        load_chunk(0)
        load_chunk(1)
        load_chunk(2)
        load_pw(0)
        load_chunk(3)
        for u in range(HEAD_UNITS):
            unit_front(u, u % 3)
            if 0 < u < HEAD_UNITS - 1:
                unit_back(u - 1)
            if u >= HEAD_UNITS - 2:
                unit_back(u)
            if u == 3:
                load_pw(1)
        g_ps = broadcast_g(0)
        broadcast_b(0, 1)
        broadcast_b(0, 0)
        make_cb(0)
        waiting = []

        for s in range(N_SLOTS):
            n, i = divmod(s, 8)
            cd_w, sc_w = codes[(n, 0)]
            cd_a, sc_a = codes[(n, 1)]
            rows = slice(P * i, P * i + P)
            xs = xsp.tile([P, D], F32, name="xs%d" % s, tag="xs")
            sums = smallp.tile([P, 2], F32, name="sums%d" % s, tag="sums")
            x_ps = []
            for h in range(2):
                cols = slice(H * h, H * h + H)
                x_h = psum_x.tile([P, H], F32, name="x", tag="x")
                for g in range(2):
                    nc.tensor.matmul_mx(
                        out=x_h[:],
                        lhsT=cd_a[:, g, rows].bitcast(FP8X4),
                        lhsT_scale=sc_a[:, g, rows],
                        rhs=cd_w[:, g, cols].bitcast(FP8X4),
                        rhs_scale=sc_w[:, g, cols],
                        start=(g == 0),
                        stop=(g == 1),
                    )
                x_ps.append(x_h)
            if s == 0:
                for e in EARLY_C_SLOTS:
                    make_ca(e)
            nc.scalar.activation(out=xs[:, 0:H], in_=x_ps[0][:], func=ACT.Copy, accum_out=sums[:, 0:1])
            if s > 0:
                make_rstd(s - 1)
            nc.scalar.activation(out=xs[:, H:D], in_=x_ps[1][:], func=ACT.Copy, accum_out=sums[:, 1:2])
            if s > 0:
                finish_b(s - 1)
            for u in waiting:
                unit_back(u)
            if s + 1 < N_SLOTS:
                make_cb(s + 1)
                if s + 1 not in PE_C_SLOTS and s + 1 not in EARLY_C_SLOTS:
                    make_ca(s + 1)
            if s > 0:
                if s - 1 in PE_C_SLOTS:
                    make_c_pe(s - 1)
                finish_a(s - 1)
            waiting = units_of_slot(s)
            for k, u in enumerate(waiting):
                unit_front(u, 2 * k)
            if s > 0 and i == 0:
                g_ps = broadcast_g(n)
            negmean = smallp.tile([P, 1], F32, name="nm%d" % s, tag="nm")
            nc.scalar.activation(out=junk2[:], in_=sums[:], func=ACT.Copy, scale=-1.0 / D, accum_out=negmean[:])
            t_t = tpool.tile([P, D], F32, name="t%d" % s, tag="t")
            for h in (1, 0):
                cols = slice(H * h, H * h + H)
                nc.vector.scalar_tensor_tensor(
                    out=t_t[:, cols], in0=xs[:, cols], scalar=negmean[:], in1=g_ps[h][:], op0=ALU.add, op1=ALU.mult
                )
            ssq = smallp.tile([P, 1], F32, name="ssq%d" % s, tag="ssq")
            nc.scalar.activation(out=junk[:], in_=xs[:], func=ACT.Square, bias=negmean[:], scale=1.0, accum_out=ssq[:])
            state[s] = (t_t, ssq)
            if s in B_SLOTS:
                broadcast_b(B_SLOTS[s][0], B_SLOTS[s][1])
            if s == 1:
                load_pw(2)
            if s >= 4 and s % 4 == 0 and s // 4 + 2 < 2 * NB:
                load_pw(s // 4 + 2)
        make_rstd(N_SLOTS - 1)
        finish_b(N_SLOTS - 1)
        finish_a(N_SLOTS - 1)
